import numpy as np
import ml_dtypes

BF16 = ml_dtypes.bfloat16


def bf(x):
    return np.asarray(x, np.float32).astype(BF16)


def f32(x):
    return np.asarray(x, np.float32)


def f64(x):
    return np.asarray(x).astype(np.float64)


def striped(idx):
    return np.tile(idx.reshape(-1, 16).T, (8, 1))


D, S, T, N = 128, 2048, 1024, 512


def setup_inputs():
    return {"queries": bf(np.random.standard_normal((D, S))), "keys": bf(np.random.standard_normal((D, T))), "wq": bf(0.5 * np.random.standard_normal((D, D)) / np.sqrt(D)), "bq": f32(0.1 * np.random.standard_normal((D, 1))), "wk": bf(0.5 * np.random.standard_normal((D, D)) / np.sqrt(D)), "bk": f32(0.1 * np.random.standard_normal((D, 1))), "offs": striped(np.random.permutation(S)[:N])}


def reference(queries, keys, wq, bq, wk, bk, offs):
    idx = offs[:16].T.reshape(-1)
    q = f64(wq).T @ f64(queries)[:, idx] + f64(bq)
    k = f64(wk).T @ f64(keys) + f64(bk)
    return k.T @ q

@@ -1,0 +1,55 @@
+import concourse.mybir as mybir
+
+P = 128
+S = 2048
+T = 1024
+N = 512
+FLOPS = 2 * P * P * N + 2 * P * P * T + 2 * P * T * N
+
+BF16, F32, U16 = mybir.dt.bfloat16, mybir.dt.float32, mybir.dt.uint16
+IDENTITY = mybir.ActivationFunctionType.Identity
+
+
+def tile_trendattentionlayer_kernel(tc, queries, keys, wq, bq, wk, bk, offs, out):
+    nc = tc.nc
+    with (
+        tc.tile_pool(name="held", bufs=1) as held,
+        tc.tile_pool(name="staged", bufs=T // P) as staged,
+        tc.psum_pool(name="proj", bufs=1) as proj,
+        tc.psum_pool(name="scores", bufs=4) as scores,
+    ):
+        offsets = held.tile([P, N // 16], U16, name="offsets")
+        nc.sync.dma_start(offsets[:], offs)
+        wq_sb = held.tile([P, P], BF16, name="wq_sb")
+        nc.sync.dma_start(wq_sb[:], wq)
+        store = held.tile([P, S], BF16, name="store")
+        nc.sync.dma_start(store[:], queries)
+        wk_sb = held.tile([P, P], BF16, name="wk_sb")
+        nc.scalar.dma_start(wk_sb[:], wk)
+        keys_sb = held.tile([P, T], BF16, name="keys_sb")
+        nc.scalar.dma_start(keys_sb[:], keys)
+        bq_sb = held.tile([P, 1], F32, name="bq_sb")
+        nc.gpsimd.dma_start(bq_sb[:], bq)
+        bk_sb = held.tile([P, 1], F32, name="bk_sb")
+        nc.gpsimd.dma_start(bk_sb[:], bk)
+
+        k_sb = held.tile([P, T], BF16, name="k_sb")
+        for h in range(T // N):
+            k_ps = proj.tile([P, N], F32, name=f"k_ps{h}")
+            nc.tensor.matmul(k_ps[:], wk_sb[:], keys_sb[:, h * N : (h + 1) * N], start=True, stop=True)
+            nc.scalar.activation(k_sb[:, h * N : (h + 1) * N], k_ps[:], IDENTITY, bias=bk_sb[:])
+
+        q_ps = proj.tile([P, N], F32, name="q_ps")
+        nc.tensor.matmul(q_ps[:], wq_sb[:], store[:].indirect(offsets[:]), start=True, stop=True)
+        q_sb = held.tile([P, N], BF16, name="q_sb")
+        nc.vector.tensor_scalar_add(q_sb[:], q_ps[:], bq_sb[:])
+
+        for b in range(T // P):
+            block_ps = scores.tile([P, N], F32, name="block_ps")
+            nc.tensor.matmul(block_ps[:], k_sb[:, b * P : (b + 1) * P], q_sb[:], start=True, stop=True)
+            block_sb = staged.tile([P, N], F32, name="block_sb")
+            if b % 2 == 0:
+                nc.vector.tensor_copy(block_sb[:], block_ps[:])
+            else:
+                nc.scalar.copy(block_sb[:], block_ps[:])
+            nc.sync.dma_start(out[b * P : (b + 1) * P, :], block_sb[:])

@@ -4,6 +4,7 @@ P = 128
 S = 2048
 T = 1024
 N = 512
+H = N // 2
 FLOPS = 2 * P * P * N + 2 * P * P * T + 2 * P * T * N
 
 BF16, F32, U16 = mybir.dt.bfloat16, mybir.dt.float32, mybir.dt.uint16
@@ -15,41 +16,63 @@ def tile_trendattentionlayer_kernel(tc, queries, keys, wq, bq, wk, bk, offs, out
     with (
         tc.tile_pool(name="held", bufs=1) as held,
         tc.tile_pool(name="staged", bufs=T // P) as staged,
-        tc.psum_pool(name="proj", bufs=1) as proj,
-        tc.psum_pool(name="scores", bufs=4) as scores,
+        tc.psum_pool(name="proj", bufs=2) as proj,
+        tc.psum_pool(name="scores", bufs=2) as scores,
     ):
         offsets = held.tile([P, N // 16], U16, name="offsets")
         nc.sync.dma_start(offsets[:], offs)
+        bq_sb = held.tile([P, 1], F32, name="bq_sb")
+        nc.sync.dma_start(bq_sb[:], bq)
+        bk_sb = held.tile([P, 1], F32, name="bk_sb")
+        nc.scalar.dma_start(bk_sb[:], bk)
         wq_sb = held.tile([P, P], BF16, name="wq_sb")
-        nc.sync.dma_start(wq_sb[:], wq)
+        nc.scalar.dma_start(wq_sb[:], wq)
         store = held.tile([P, S], BF16, name="store")
-        nc.sync.dma_start(store[:], queries)
+        for c in range(S // N):
+            queue = nc.sync if c % 2 == 0 else nc.scalar
+            queue.dma_start(store[:, c * N : (c + 1) * N], queries[:, c * N : (c + 1) * N])
         wk_sb = held.tile([P, P], BF16, name="wk_sb")
         nc.scalar.dma_start(wk_sb[:], wk)
         keys_sb = held.tile([P, T], BF16, name="keys_sb")
-        nc.scalar.dma_start(keys_sb[:], keys)
-        bq_sb = held.tile([P, 1], F32, name="bq_sb")
-        nc.gpsimd.dma_start(bq_sb[:], bq)
-        bk_sb = held.tile([P, 1], F32, name="bk_sb")
-        nc.gpsimd.dma_start(bk_sb[:], bk)
+        for c in range(T // N):
+            queue = nc.sync if c % 2 == 0 else nc.scalar
+            queue.dma_start(keys_sb[:, c * N : (c + 1) * N], keys[:, c * N : (c + 1) * N])
+
+
+        q_sb = held.tile([P, N], BF16, name="q_sb")
+        for half in range(N // H):
+            q_ps = proj.tile([P, H], F32, name="q_ps")
+            picked = store[:].indirect(offsets[:, half * H // 16 : (half + 1) * H // 16])
+            nc.tensor.matmul(q_ps[:], wq_sb[:], picked, start=True, stop=True)
+            if half % 2 == 0:
+                nc.vector.tensor_scalar_add(q_sb[:, half * H : (half + 1) * H], q_ps[:], bq_sb[:])
+            else:
+                nc.scalar.activation(q_sb[:, half * H : (half + 1) * H], q_ps[:], IDENTITY, bias=bq_sb[:])
 
         k_sb = held.tile([P, T], BF16, name="k_sb")
-        for h in range(T // N):
-            k_ps = proj.tile([P, N], F32, name=f"k_ps{h}")
-            nc.tensor.matmul(k_ps[:], wk_sb[:], keys_sb[:, h * N : (h + 1) * N], start=True, stop=True)
-            nc.scalar.activation(k_sb[:, h * N : (h + 1) * N], k_ps[:], IDENTITY, bias=bk_sb[:])
 
-        q_ps = proj.tile([P, N], F32, name="q_ps")
-        nc.tensor.matmul(q_ps[:], wq_sb[:], store[:].indirect(offsets[:]), start=True, stop=True)
-        q_sb = held.tile([P, N], BF16, name="q_sb")
-        nc.vector.tensor_scalar_add(q_sb[:], q_ps[:], bq_sb[:])
-
-        for b in range(T // P):
-            block_ps = scores.tile([P, N], F32, name="block_ps")
-            nc.tensor.matmul(block_ps[:], k_sb[:, b * P : (b + 1) * P], q_sb[:], start=True, stop=True)
-            block_sb = staged.tile([P, N], F32, name="block_sb")
-            if b % 2 == 0:
-                nc.vector.tensor_copy(block_sb[:], block_ps[:])
+        def project_keys(c):
+            k_ps = proj.tile([P, H], F32, name="k_ps")
+            nc.tensor.matmul(k_ps[:], wk_sb[:], keys_sb[:, c * H : (c + 1) * H], start=True, stop=True)
+            if c % 2 == 0:
+                nc.vector.tensor_scalar_add(k_sb[:, c * H : (c + 1) * H], k_ps[:], bk_sb[:])
             else:
-                nc.scalar.copy(block_sb[:], block_ps[:])
+                nc.scalar.activation(k_sb[:, c * H : (c + 1) * H], k_ps[:], IDENTITY, bias=bk_sb[:])
+
+        def score_block(b):
+            k_block = k_sb[:, b * P : (b + 1) * P]
+            left_ps = scores.tile([P, H], F32, name="left_ps")
+            nc.tensor.matmul(left_ps[:], k_block, q_sb[:, :H], start=True, stop=True)
+            right_ps = scores.tile([P, H], F32, name="right_ps")
+            nc.tensor.matmul(right_ps[:], k_block, q_sb[:, H:], start=True, stop=True)
+            block_sb = staged.tile([P, N], F32, name="block_sb")
+            nc.vector.tensor_copy(block_sb[:, :H], left_ps[:])
+            nc.scalar.copy(block_sb[:, H:], right_ps[:])
             nc.sync.dma_start(out[b * P : (b + 1) * P, :], block_sb[:])
+
+        project_keys(0)
+        for c in range(T // H):
+            if c + 1 < T // H:
+                project_keys(c + 1)
+            for b in range(c * H // P, (c + 1) * H // P):
+                score_block(b)

@@ -5,6 +5,7 @@ S = 2048
 T = 1024
 N = 512
 H = N // 2
+WARM = 6
 FLOPS = 2 * P * P * N + 2 * P * P * T + 2 * P * T * N
 
 BF16, F32, U16 = mybir.dt.bfloat16, mybir.dt.float32, mybir.dt.uint16
@@ -37,6 +38,12 @@ def tile_trendattentionlayer_kernel(tc, queries, keys, wq, bq, wk, bk, offs, out
         for c in range(T // N):
             queue = nc.sync if c % 2 == 0 else nc.scalar
             queue.dma_start(keys_sb[:, c * N : (c + 1) * N], keys[:, c * N : (c + 1) * N])
+
+        zeros = held.tile([P, N], BF16, name="zeros")
+        nc.vector.memset(zeros[:], 0.0)
+        warm_ps = scores.tile([P, N], F32, name="warm_ps", tag="left_ps")
+        for i in range(WARM):
+            nc.tensor.matmul(warm_ps[:], zeros[:, :P], zeros[:], start=True, stop=True)
 
 
         q_sb = held.tile([P, N], BF16, name="q_sb")

@@ -22,22 +22,18 @@ def tile_trendattentionlayer_kernel(tc, queries, keys, wq, bq, wk, bk, offs, out
     ):
         offsets = held.tile([P, N // 16], U16, name="offsets")
         nc.sync.dma_start(offsets[:], offs)
-        bq_sb = held.tile([P, 1], F32, name="bq_sb")
-        nc.sync.dma_start(bq_sb[:], bq)
-        bk_sb = held.tile([P, 1], F32, name="bk_sb")
-        nc.scalar.dma_start(bk_sb[:], bk)
+        store = held.tile([P, S], BF16, name="store")
+        nc.sync.dma_start(store[:], queries)
+        keys_sb = held.tile([P, T], BF16, name="keys_sb")
+        nc.sync.dma_start(keys_sb[:], keys)
         wq_sb = held.tile([P, P], BF16, name="wq_sb")
         nc.scalar.dma_start(wq_sb[:], wq)
-        store = held.tile([P, S], BF16, name="store")
-        for c in range(S // N):
-            queue = nc.sync if c % 2 == 0 else nc.scalar
-            queue.dma_start(store[:, c * N : (c + 1) * N], queries[:, c * N : (c + 1) * N])
+        bq_sb = held.tile([P, 1], F32, name="bq_sb")
+        nc.scalar.dma_start(bq_sb[:], bq)
         wk_sb = held.tile([P, P], BF16, name="wk_sb")
         nc.scalar.dma_start(wk_sb[:], wk)
-        keys_sb = held.tile([P, T], BF16, name="keys_sb")
-        for c in range(T // N):
-            queue = nc.sync if c % 2 == 0 else nc.scalar
-            queue.dma_start(keys_sb[:, c * N : (c + 1) * N], keys[:, c * N : (c + 1) * N])
+        bk_sb = held.tile([P, 1], F32, name="bk_sb")
+        nc.scalar.dma_start(bk_sb[:], bk)
 
         zeros = held.tile([P, N], BF16, name="zeros")
         nc.vector.memset(zeros[:], 0.0)

@@ -5,6 +5,7 @@ S = 2048
 T = 1024
 N = 512
 H = N // 2
+BANKS = 8
 WARM = 6
 FLOPS = 2 * P * P * N + 2 * P * P * T + 2 * P * T * N
 
@@ -17,8 +18,7 @@ def tile_trendattentionlayer_kernel(tc, queries, keys, wq, bq, wk, bk, offs, out
     with (
         tc.tile_pool(name="held", bufs=1) as held,
         tc.tile_pool(name="staged", bufs=T // P) as staged,
-        tc.psum_pool(name="proj", bufs=2) as proj,
-        tc.psum_pool(name="scores", bufs=2) as scores,
+        tc.psum_pool(name="psum", bufs=BANKS) as psum,
     ):
         offsets = held.tile([P, N // 16], U16, name="offsets")
         nc.sync.dma_start(offsets[:], offs)
@@ -37,14 +37,17 @@ def tile_trendattentionlayer_kernel(tc, queries, keys, wq, bq, wk, bk, offs, out
 
         zeros = held.tile([P, N], BF16, name="zeros")
         nc.vector.memset(zeros[:], 0.0)
-        warm_ps = scores.tile([P, N], F32, name="warm_ps", tag="left_ps")
+        warm_ps = psum.tile([P, N], F32, name="warm_ps", tag="bank")
         for i in range(WARM):
             nc.tensor.matmul(warm_ps[:], zeros[:, :P], zeros[:], start=True, stop=True)
+
+        scratch = held.tile([P, 1], F32, name="scratch")
+        nc.scalar.activation(scratch[:], zeros[:, :1], IDENTITY)
 
 
         q_sb = held.tile([P, N], BF16, name="q_sb")
         for half in range(N // H):
-            q_ps = proj.tile([P, H], F32, name="q_ps")
+            q_ps = psum.tile([P, H], F32, name="q_ps", tag="bank")
             picked = store[:].indirect(offsets[:, half * H // 16 : (half + 1) * H // 16])
             nc.tensor.matmul(q_ps[:], wq_sb[:], picked, start=True, stop=True)
             if half % 2 == 0:
@@ -55,7 +58,7 @@ def tile_trendattentionlayer_kernel(tc, queries, keys, wq, bq, wk, bk, offs, out
         k_sb = held.tile([P, T], BF16, name="k_sb")
 
         def project_keys(c):
-            k_ps = proj.tile([P, H], F32, name="k_ps")
+            k_ps = psum.tile([P, H], F32, name="k_ps", tag="bank")
             nc.tensor.matmul(k_ps[:], wk_sb[:], keys_sb[:, c * H : (c + 1) * H], start=True, stop=True)
             if c % 2 == 0:
                 nc.vector.tensor_scalar_add(k_sb[:, c * H : (c + 1) * H], k_ps[:], bk_sb[:])
@@ -64,9 +67,9 @@ def tile_trendattentionlayer_kernel(tc, queries, keys, wq, bq, wk, bk, offs, out
 
         def score_block(b):
             k_block = k_sb[:, b * P : (b + 1) * P]
-            left_ps = scores.tile([P, H], F32, name="left_ps")
+            left_ps = psum.tile([P, H], F32, name="left_ps", tag="bank")
             nc.tensor.matmul(left_ps[:], k_block, q_sb[:, :H], start=True, stop=True)
-            right_ps = scores.tile([P, H], F32, name="right_ps")
+            right_ps = psum.tile([P, H], F32, name="right_ps", tag="bank")
             nc.tensor.matmul(right_ps[:], k_block, q_sb[:, H:], start=True, stop=True)
             block_sb = staged.tile([P, N], F32, name="block_sb")
             nc.vector.tensor_copy(block_sb[:, :H], left_ps[:])

@@ -41,9 +41,6 @@ def tile_trendattentionlayer_kernel(tc, queries, keys, wq, bq, wk, bk, offs, out
         for i in range(WARM):
             nc.tensor.matmul(warm_ps[:], zeros[:, :P], zeros[:], start=True, stop=True)
 
-        scratch = held.tile([P, 1], F32, name="scratch")
-        nc.scalar.activation(scratch[:], zeros[:, :1], IDENTITY)
-
 
         q_sb = held.tile([P, N], BF16, name="q_sb")
         for half in range(N // H):

@@ -6,7 +6,7 @@ T = 1024
 N = 512
 H = N // 2
 BANKS = 8
-WARM = 6
+WARM = 4
 FLOPS = 2 * P * P * N + 2 * P * P * T + 2 * P * T * N
 
 BF16, F32, U16 = mybir.dt.bfloat16, mybir.dt.float32, mybir.dt.uint16

@@ -71,7 +71,11 @@ def tile_trendattentionlayer_kernel(tc, queries, keys, wq, bq, wk, bk, offs, out
             block_sb = staged.tile([P, N], F32, name="block_sb")
             nc.vector.tensor_copy(block_sb[:, :H], left_ps[:])
             nc.scalar.copy(block_sb[:, H:], right_ps[:])
-            nc.sync.dma_start(out[b * P : (b + 1) * P, :], block_sb[:])
+            if b == 0:
+                nc.sync.dma_start(out[b * P : (b + 1) * P, :H], block_sb[:, :H])
+                nc.sync.dma_start(out[b * P : (b + 1) * P, H:], block_sb[:, H:])
+            else:
+                nc.sync.dma_start(out[b * P : (b + 1) * P, :], block_sb[:])
 
         project_keys(0)
         for c in range(T // H):

@@ -18,6 +18,7 @@ def tile_trendattentionlayer_kernel(tc, queries, keys, wq, bq, wk, bk, offs, out
     with (
         tc.tile_pool(name="held", bufs=1) as held,
         tc.tile_pool(name="staged", bufs=T // P) as staged,
+        tc.tile_pool(name="last", bufs=1) as last,
         tc.psum_pool(name="psum", bufs=BANKS) as psum,
     ):
         offsets = held.tile([P, N // 16], U16, name="offsets")
@@ -40,6 +41,8 @@ def tile_trendattentionlayer_kernel(tc, queries, keys, wq, bq, wk, bk, offs, out
         warm_ps = psum.tile([P, N], F32, name="warm_ps", tag="bank")
         for i in range(WARM):
             nc.tensor.matmul(warm_ps[:], zeros[:, :P], zeros[:], start=True, stop=True)
+        unused = last.tile([P, 1], F32, name="unused")
+        nc.scalar.activation(unused[:], zeros[:, :1], IDENTITY, bias=zeros[:, :1])
 
 
         q_sb = held.tile([P, N], BF16, name="q_sb")
@@ -53,14 +56,23 @@ def tile_trendattentionlayer_kernel(tc, queries, keys, wq, bq, wk, bk, offs, out
                 nc.scalar.activation(q_sb[:, half * H : (half + 1) * H], q_ps[:], IDENTITY, bias=bq_sb[:])
 
         k_sb = held.tile([P, T], BF16, name="k_sb")
+        bounds = [0, P] + list(range(H, T + 1, H))
+        pieces = list(zip(bounds, bounds[1:]))
+        banks = {}
 
         def project_keys(c):
+            first, last = pieces[c]
             k_ps = psum.tile([P, H], F32, name="k_ps", tag="bank")
-            nc.tensor.matmul(k_ps[:], wk_sb[:], keys_sb[:, c * H : (c + 1) * H], start=True, stop=True)
+            nc.tensor.matmul(k_ps[:, : last - first], wk_sb[:], keys_sb[:, first:last], start=True, stop=True)
+            banks[c] = k_ps
+
+        def keep_keys(c):
+            first, last = pieces[c]
+            k_ps = banks[c]
             if c % 2 == 0:
-                nc.vector.tensor_scalar_add(k_sb[:, c * H : (c + 1) * H], k_ps[:], bk_sb[:])
+                nc.vector.tensor_scalar_add(k_sb[:, first:last], k_ps[:, : last - first], bk_sb[:])
             else:
-                nc.scalar.activation(k_sb[:, c * H : (c + 1) * H], k_ps[:], IDENTITY, bias=bk_sb[:])
+                nc.scalar.activation(k_sb[:, first:last], k_ps[:, : last - first], IDENTITY, bias=bk_sb[:])
 
         def score_block(b):
             k_block = k_sb[:, b * P : (b + 1) * P]
@@ -78,8 +90,13 @@ def tile_trendattentionlayer_kernel(tc, queries, keys, wq, bq, wk, bk, offs, out
                 nc.sync.dma_start(out[b * P : (b + 1) * P, :], block_sb[:])
 
         project_keys(0)
-        for c in range(T // H):
-            if c + 1 < T // H:
-                project_keys(c + 1)
-            for b in range(c * H // P, (c + 1) * H // P):
-                score_block(b)
+        project_keys(1)
+        keep_keys(0)
+        keep_keys(1)
+        for c in range(2, len(pieces) + 1):
+            if c < len(pieces):
+                project_keys(c)
+            score_block(2 * c - 4)
+            if c < len(pieces):
+                keep_keys(c)
+            score_block(2 * c - 3)

import concourse.mybir as mybir

P = 128
S = 2048
T = 1024
N = 512
H = N // 2
BANKS = 8
WARM = 4
FLOPS = 2 * P * P * N + 2 * P * P * T + 2 * P * T * N

BF16, F32, U16 = mybir.dt.bfloat16, mybir.dt.float32, mybir.dt.uint16
IDENTITY = mybir.ActivationFunctionType.Identity


def tile_trendattentionlayer_kernel(tc, queries, keys, wq, bq, wk, bk, offs, out):
    nc = tc.nc
    with (
        tc.tile_pool(name="held", bufs=1) as held,
        tc.tile_pool(name="staged", bufs=T // P) as staged,
        tc.tile_pool(name="last", bufs=1) as last,
        tc.psum_pool(name="psum", bufs=BANKS) as psum,
    ):
        offsets = held.tile([P, N // 16], U16, name="offsets")
        nc.sync.dma_start(offsets[:], offs)
        store = held.tile([P, S], BF16, name="store")
        nc.sync.dma_start(store[:], queries)
        keys_sb = held.tile([P, T], BF16, name="keys_sb")
        nc.sync.dma_start(keys_sb[:], keys)
        wq_sb = held.tile([P, P], BF16, name="wq_sb")
        nc.scalar.dma_start(wq_sb[:], wq)
        bq_sb = held.tile([P, 1], F32, name="bq_sb")
        nc.scalar.dma_start(bq_sb[:], bq)
        wk_sb = held.tile([P, P], BF16, name="wk_sb")
        nc.scalar.dma_start(wk_sb[:], wk)
        bk_sb = held.tile([P, 1], F32, name="bk_sb")
        nc.scalar.dma_start(bk_sb[:], bk)

        zeros = held.tile([P, N], BF16, name="zeros")
        nc.vector.memset(zeros[:], 0.0)
        warm_ps = psum.tile([P, N], F32, name="warm_ps", tag="bank")
        for i in range(WARM):
            nc.tensor.matmul(warm_ps[:], zeros[:, :P], zeros[:], start=True, stop=True)
        unused = last.tile([P, 1], F32, name="unused")
        nc.scalar.activation(unused[:], zeros[:, :1], IDENTITY, bias=zeros[:, :1])


        q_sb = held.tile([P, N], BF16, name="q_sb")
        for half in range(N // H):
            q_ps = psum.tile([P, H], F32, name="q_ps", tag="bank")
            picked = store[:].indirect(offsets[:, half * H // 16 : (half + 1) * H // 16])
            nc.tensor.matmul(q_ps[:], wq_sb[:], picked, start=True, stop=True)
            if half % 2 == 0:
                nc.vector.tensor_scalar_add(q_sb[:, half * H : (half + 1) * H], q_ps[:], bq_sb[:])
            else:
                nc.scalar.activation(q_sb[:, half * H : (half + 1) * H], q_ps[:], IDENTITY, bias=bq_sb[:])

        k_sb = held.tile([P, T], BF16, name="k_sb")
        bounds = [0, P] + list(range(H, T + 1, H))
        pieces = list(zip(bounds, bounds[1:]))
        banks = {}

        def project_keys(c):
            first, last = pieces[c]
            k_ps = psum.tile([P, H], F32, name="k_ps", tag="bank")
            nc.tensor.matmul(k_ps[:, : last - first], wk_sb[:], keys_sb[:, first:last], start=True, stop=True)
            banks[c] = k_ps

        def keep_keys(c):
            first, last = pieces[c]
            k_ps = banks[c]
            if c % 2 == 0:
                nc.vector.tensor_scalar_add(k_sb[:, first:last], k_ps[:, : last - first], bk_sb[:])
            else:
                nc.scalar.activation(k_sb[:, first:last], k_ps[:, : last - first], IDENTITY, bias=bk_sb[:])

        def score_block(b):
            k_block = k_sb[:, b * P : (b + 1) * P]
            left_ps = psum.tile([P, H], F32, name="left_ps", tag="bank")
            nc.tensor.matmul(left_ps[:], k_block, q_sb[:, :H], start=True, stop=True)
            right_ps = psum.tile([P, H], F32, name="right_ps", tag="bank")
            nc.tensor.matmul(right_ps[:], k_block, q_sb[:, H:], start=True, stop=True)
            block_sb = staged.tile([P, N], F32, name="block_sb")
            nc.vector.tensor_copy(block_sb[:, :H], left_ps[:])
            nc.scalar.copy(block_sb[:, H:], right_ps[:])
            if b == 0:
                nc.sync.dma_start(out[b * P : (b + 1) * P, :H], block_sb[:, :H])
                nc.sync.dma_start(out[b * P : (b + 1) * P, H:], block_sb[:, H:])
            else:
                nc.sync.dma_start(out[b * P : (b + 1) * P, :], block_sb[:])

        project_keys(0)
        project_keys(1)
        keep_keys(0)
        keep_keys(1)
        for c in range(2, len(pieces) + 1):
            if c < len(pieces):
                project_keys(c)
            score_block(2 * c - 4)
            if c < len(pieces):
                keep_keys(c)
            score_block(2 * c - 3)
